import numpy as np
import ml_dtypes


def mxq(x, axis, fmt="e4m3"):
    dtype, down = {"e4m3": (ml_dtypes.float8_e4m3fn, 7), "e5m2": (ml_dtypes.float8_e5m2, 14)}[fmt]
    v = np.moveaxis(np.asarray(x, np.float32).astype(ml_dtypes.bfloat16).astype(np.float64), axis, -1)
    blocks = v.reshape(v.shape[:-1] + (-1, 32))
    amax = np.abs(blocks).max(-1, keepdims=True)
    byte = np.maximum(np.where(amax > 0, np.frexp(amax)[1] - 1 + 127, 0) - down, 1)
    scale = np.exp2(byte - 127.0)
    codes = (blocks / scale).astype(np.float32).astype(dtype).astype(np.float64)
    return np.moveaxis((codes * scale).reshape(v.shape), -1, axis)


WIDE = False


def mx_kscale(k):
    if not WIDE:
        return np.ones(k)
    levels = np.array([10, -10, 5, -5, 0])
    if k % 512:
        return np.exp2(np.random.permutation(np.resize(levels, k // 32))).repeat(32)
    a = np.empty((k // 512, 16))
    for p in range(k // 512):
        a[p, :8] = np.random.permutation(np.resize(levels, 8))
        for g in range(8):
            far = levels[np.abs(levels - a[p, g]) >= 10]
            a[p, g + 8] = far[np.random.randint(len(far))]
    return np.exp2(a.ravel()).repeat(32)


BF16 = ml_dtypes.bfloat16


def bf(x):
    return np.asarray(x, np.float32).astype(BF16)


def f64(x):
    return np.asarray(x).astype(np.float64)


E2M1 = np.array([0.0, 0.5, 1.0, 1.5, 2.0, 3.0, 4.0, 6.0, -0.0, -0.5, -1.0, -1.5, -2.0, -3.0, -4.0, -6.0])


def pack_weight(w, fmt):
    k, n = w.shape
    w = f64(bf(w)).reshape(k // 32, 32, n)
    amax = np.abs(w).max(1)
    if fmt == "e4m3":
        byte = np.frexp(amax)[1] - 1 + 127 - 7
    else:
        mant, ex = np.frexp(amax / 6.0)
        byte = np.where(mant > 0.5, ex, ex - 1) + 127
    byte = np.clip(np.where(amax > 0, byte, 1), 1, 254)
    scaled = (w * np.exp2(127.0 - byte)[:, None, :]).reshape(k, n).astype(np.float32)
    by_word = np.ascontiguousarray(scaled.reshape(k // 512, 128, 4, n).transpose(0, 1, 3, 2))
    if fmt == "e4m3":
        words = by_word.astype(ml_dtypes.float8_e4m3fn).view(np.uint8)
    else:
        c = by_word.astype(ml_dtypes.float4_e2m1fn).view(np.uint8) & 0xF
        words = c[..., 0::2] | (c[..., 1::2] << 4)
    return np.ascontiguousarray(words), np.ascontiguousarray(byte.astype(np.uint8).reshape(k // 512, 16, n))


def unpack_weight(words, scales, fmt):
    g, p, n, _ = words.shape
    if fmt == "e4m3":
        vals = np.ascontiguousarray(words).view(ml_dtypes.float8_e4m3fn).astype(np.float64)
    else:
        nib = np.empty((g, p, n, 4), np.uint8)
        nib[..., 0::2] = words & 0xF
        nib[..., 1::2] = words >> 4
        vals = E2M1[nib]
    vals = vals * np.repeat(np.exp2(scales.astype(np.float64) - 127.0), 8, axis=1)[..., None]
    return vals.transpose(0, 1, 3, 2).reshape(g * 512, n)
def pack4(w):
    words, scales = pack_weight(w, "e2m1")
    return words.reshape(words.shape[0], 128, -1), scales


def unpack4(words, scales):
    return unpack_weight(words.reshape(words.shape[0], 128, -1, 2), scales, "e2m1")


B, C, H, W = 4, 512, 32, 32
C2 = 2 * C
N = H * W


def sigmoid(v):
    return 1.0 / (1.0 + np.exp(-v))


def draw0():
    s = mx_kscale(C2)
    t = mx_kscale(C)
    hsi = bf(np.random.standard_normal((B, C, H, W)) * s[:C][None, :, None, None])
    msi = bf(np.random.standard_normal((B, C, H, W)) * s[C:][None, :, None, None])
    att1 = bf(np.random.standard_normal((B, C, H, W)) * 0.5 * t[None, :, None, None])
    att2 = bf(np.random.standard_normal((B, C, H, W)) * 0.5 * t[None, :, None, None])
    wg = np.random.standard_normal((C, C2)) / np.sqrt(C2) / s[None, :]
    wg_words, wg_scales = pack4(wg.T)
    bg = bf(np.random.standard_normal(C) * 0.2)
    wp = np.random.standard_normal((C, C)) * 2.0 / np.sqrt(C) / t[None, :]
    wp_words, wp_scales = pack4(wp.T)
    bp = bf(np.random.standard_normal(C) * 0.1)
    return {"hsi": hsi,
            "msi": msi,
            "att1": att1,
            "att2": att2,
            "wg_words": wg_words,
            "wg_scales": wg_scales,
            "bg": bg,
            "wp_words": wp_words,
            "wp_scales": wp_scales,
            "bp": bp}


def core(hsi, msi, att1, att2, wg_words, wg_scales, bg, wp_words, wp_scales, bp):
    x = np.concatenate([f64(hsi), f64(msi)], axis=1).reshape(B, C2, N)
    g = sigmoid((unpack4(wg_words, wg_scales).T @ mxq(x, 1, "e4m3")) + f64(bg)[None, :, None])
    fused = g * f64(att1).reshape(B, C, N) + (1.0 - g) * f64(att2).reshape(B, C, N)
    y = (unpack4(wp_words, wp_scales).T @ mxq(fused, 1, "e4m3")) + f64(bp)[None, :, None]
    return y.reshape(B, C, H, W)


def e4m3fn_bytes(y):
    return np.clip(np.asarray(y, np.float64), -448.0, 448.0).astype(np.float32).astype(ml_dtypes.float8_e4m3fn).view(np.uint8)


def e4m3fn_values(b):
    return np.asarray(b, np.uint8).view(ml_dtypes.float8_e4m3fn).astype(np.float64)


def setup_inputs():
    d = draw0()
    x0 = np.asarray(d['msi']).astype(np.float64)
    s = (np.max(np.abs(x0), axis=(0, 2, 3), keepdims=True) / 448.0).astype(np.float32)
    out = {}
    for k, v in d.items():
        if k == 'msi':
            out['msi_bytes'] = e4m3fn_bytes(x0 / s.astype(np.float64))
            out['msi_scale'] = s
        else:
            out[k] = v
    return out


def reference(hsi, msi_bytes, msi_scale, att1, att2, wg_words, wg_scales, bg, wp_words, wp_scales, bp):
    return core(hsi, e4m3fn_values(msi_bytes) * msi_scale.astype(np.float64), att1, att2, wg_words, wg_scales, bg, wp_words, wp_scales, bp)

@@ -1,0 +1,292 @@
+from contextlib import ExitStack
+
+import concourse.mybir as mybir
+from concourse.masks import make_identity
+
+BF16 = mybir.dt.bfloat16
+F32 = mybir.dt.float32
+I32 = mybir.dt.int32
+U32 = mybir.dt.uint32
+U8 = mybir.dt.uint8
+FP8 = mybir.dt.float8_e4m3fn
+FP8X4 = mybir.dt.float8_e4m3fn_x4
+FP4X4 = mybir.dt.float4_e2m1fn_x4
+ACT = mybir.ActivationFunctionType
+ALU = mybir.AluOpType
+
+B, C, N = 4, 512, 1024
+FLOPS = 2 * B * N * (2 * C * C + C * C)
+
+P = 128
+T = 4
+W = 512
+UNITS = B * N // W
+RUN = 8
+HSI_ON_SCALAR = 512
+DIFFS_ON_TENSOR = [2, 2, 2, 2, 2, 3, 3, 3]
+
+
+def tile_crossattentionfusion_pa_t_w4_kernel(
+    tc, hsi, msi_bytes, msi_scale, att1, att2, wg_words, wg_scales, bg, wp_words, wp_scales, bp, out
+):
+    nc = tc.nc
+
+    def channels_first(x, b):
+        return x[b].rearrange("(p t) h w -> p t (h w)", t=T)
+
+    with ExitStack() as ctx:
+        keep = ctx.enter_context(tc.tile_pool(name="keep", bufs=1))
+        work = ctx.enter_context(tc.tile_pool(name="work", bufs=2))
+        gate_psum = ctx.enter_context(tc.psum_pool(name="gate_psum", bufs=3))
+        diff_psum = ctx.enter_context(tc.psum_pool(name="diff_psum", bufs=3))
+        y_psum = ctx.enter_context(tc.psum_pool(name="y_psum", bufs=2))
+        ctx.enter_context(tc.manual_schedule())
+
+        warm = keep.tile([P, 1], F32, name="warm")
+        nc.vector.memset(warm[:], 0.0)
+        nc.scalar.activation(warm[:], warm[:], ACT.Sigmoid)
+        scales_raw = keep.tile([P, 3, C], U8, name="scales_raw", align_bytes=64)
+        nc.vector.memset(scales_raw[:].rearrange("p g n -> p (g n)").bitcast(I32), 0)
+        bp_rows = keep.tile([P, P], BF16, name="bp_rows")
+        nc.gpsimd.memset(bp_rows[:], 0.0)
+        ident = keep.tile([P, P], BF16, name="ident")
+        make_identity(nc, ident[:])
+        neg_ident = keep.tile([P, P], BF16, name="neg_ident")
+        nc.vector.tensor_scalar(out=neg_ident[:], in0=ident[:], scalar1=-1.0, scalar2=None, op0=ALU.mult)
+
+        inputs = {}
+
+        def load(name, src, b, halves, dtype):
+            view = channels_first(src, b)
+            if halves is None:
+                whole = keep.tile([P, T, N], dtype, name=f"{name}_{b}")
+                nc.sync.dma_start(out=whole[:], in_=view)
+                for h in range(2):
+                    inputs[name, 2 * b + h] = whole[:, :, h * W : (h + 1) * W]
+            else:
+                for h in halves:
+                    half = keep.tile([P, T, W], dtype, name=f"{name}_{b}_{h}")
+                    nc.sync.dma_start(out=half[:], in_=view[:, :, h * W : (h + 1) * W])
+                    inputs[name, 2 * b + h] = half[:]
+
+        def load_batch(b):
+            load("msi", msi_bytes, b, None, U8)
+            load("hsi", hsi, b, None, BF16)
+            load("att1", att1, b, None, BF16)
+            load("att2", att2, b, None, BF16)
+
+        m_scale = keep.tile([P, T], F32, name="m_scale")
+        nc.sync.dma_start(out=m_scale[:], in_=msi_scale.rearrange("a (p t) b c -> p (a t b c)", t=T))
+        load("msi", msi_bytes, 0, (0,), U8)
+        wg_raw = keep.tile([P, 2, 2 * C], U8, name="wg_raw", align_bytes=64)
+        nc.sync.dma_start(out=wg_raw[:], in_=wg_words.rearrange("g p n -> p g n"))
+        load("hsi", hsi, 0, (0,), BF16)
+        for q in range(4):
+            nc.sync.dma_start(
+                out=scales_raw[32 * q : 32 * q + 4, 0:2, :].bitcast(I32),
+                in_=wg_scales[:, 4 * q : 4 * q + 4, :].rearrange("g q n -> q g n").bitcast(I32),
+            )
+        bg_raw = keep.tile([P, T], BF16, name="bg_raw")
+        nc.sync.dma_start(out=bg_raw[:], in_=bg.rearrange("(p t) -> p t", t=T))
+        load("msi", msi_bytes, 0, (1,), U8)
+        load("hsi", hsi, 0, (1,), BF16)
+        load("att1", att1, 0, (0,), BF16)
+        load("att2", att2, 0, (0,), BF16)
+        nc.sync.dma_start(out=bp_rows[0:4, :], in_=bp.rearrange("(m p) -> m p", p=P))
+        wp = keep.tile([P, 2 * C], U8, name="wp", align_bytes=64)
+        nc.sync.dma_start(out=wp[:], in_=wp_words[0])
+        for q in range(4):
+            nc.sync.dma_start(
+                out=scales_raw[32 * q : 32 * q + 4, 2, :].bitcast(I32),
+                in_=wp_scales[0, 4 * q : 4 * q + 4, :].bitcast(I32),
+            )
+        load("att1", att1, 0, (1,), BF16)
+        load("att2", att2, 0, (1,), BF16)
+        load_batch(1)
+
+        wide, inter, codes, gates, diffs, ys = {}, {}, {}, {}, {}, {}
+
+        def widen(u, t):
+            if t == 0:
+                wide[u] = work.tile([P, T, W], BF16, name="wide")
+            src = inputs["msi", u][:, t, :].bitcast(FP8)
+            if u == 0 and t >= 2:
+                nc.vector.tensor_scalar(out=wide[u][:, t, :], in0=src, scalar1=m_scale[:, t : t + 1], scalar2=None, op0=ALU.mult)
+            else:
+                nc.scalar.activation(wide[u][:, t, :], src, ACT.Copy, scale=m_scale[:, t : t + 1])
+
+        def by_runs(grouped, px):
+            return grouped.rearrange("p (c i t) -> p c t i", i=RUN, t=T)
+
+        def runs(planar):
+            return planar.rearrange("p t (c i) -> p c t i", i=RUN)
+
+        def interleave(name, u, copy, planar, lo, hi):
+            if (name, u) not in inter:
+                inter[name, u] = work.tile([P, T * W], BF16, name=f"inter_{name}", align_bytes=64)
+            copy(
+                out=by_runs(inter[name, u][:, T * lo : T * hi], hi - lo),
+                in_=runs(planar[:, :, lo:hi]),
+            )
+
+        def interleave_hsi_scalar(u):
+            if u > 0:
+                interleave("hsi", u, nc.scalar.copy, inputs["hsi", u], 0, HSI_ON_SCALAR)
+
+        def interleave_hsi_vector(u):
+            lo = HSI_ON_SCALAR if u > 0 else 0
+            if lo < W:
+                interleave("hsi", u, nc.vector.tensor_copy, inputs["hsi", u], lo, W)
+
+        def quantize(name, u, src, lo=0, hi=W):
+            if (name, u) not in codes:
+                words = work.tile([P, W], U32, name=f"codes_{name}", align_bytes=64)
+                scales = work.tile([P, W], U8, name=f"scales_{name}", align_bytes=64)
+                codes[name, u] = (words, scales)
+            words, scales = codes[name, u]
+            nc.vector.quantize_mx(out=words[:, lo:hi].bitcast(FP8X4), scales=scales[:, lo:hi], in_=src[:, T * lo : T * hi])
+
+        def gate(u, t):
+            acc = gate_psum.tile([P, W], F32, name="gate_acc")
+            for g, name in ((1, "msi"), (0, "hsi")):
+                words, scales = codes[name, u]
+                nc.tensor.matmul_mx(
+                    out=acc[:],
+                    lhsT=wg[:, g, 2 * P * t : 2 * P * (t + 1)].bitcast(FP4X4),
+                    lhsT_scale=wg_s[:, g, P * t : P * (t + 1)],
+                    rhs=words[:].bitcast(FP8X4),
+                    rhs_scale=scales[:],
+                    start=(g == 1),
+                    stop=(g == 0),
+                )
+            if t == 0:
+                gates[u] = work.tile([P, T, W], F32, name="gates")
+            nc.scalar.activation(gates[u][:, t, :], acc[:], ACT.Sigmoid, bias=bg_cols[:, t : t + 1])
+
+        def diff_tensor(u, t):
+            d = diff_psum.tile([P, W], F32, name="diff_acc")
+            nc.tensor.matmul(d[:], ident[:], inputs["att1", u][:, t, :], start=True, stop=False)
+            nc.tensor.matmul(d[:], neg_ident[:], inputs["att2", u][:, t, :], start=False, stop=True)
+            diffs[u, t] = d[:]
+
+        def diff_vector(u):
+            n = DIFFS_ON_TENSOR[u]
+            d = work.tile([P, T, W], F32, name="diff_sb")
+            nc.vector.tensor_tensor(out=d[:, n:T, :], in0=inputs["att1", u][:, n:T, :], in1=inputs["att2", u][:, n:T, :], op=ALU.subtract)
+            for t in range(n, T):
+                diffs[u, t] = d[:, t, :]
+
+        def gated(u, t):
+            g = gates[u][:, t, :]
+            nc.vector.tensor_tensor(out=g, in0=diffs[u, t], in1=g, op=ALU.mult)
+
+        def add_att2(u, lo=0, hi=W):
+            if ("fused", u) not in inter:
+                inter["fused", u] = work.tile([P, T * W], BF16, name="fused", align_bytes=64)
+            nc.vector.tensor_tensor(
+                out=by_runs(inter["fused", u][:, T * lo : T * hi], hi - lo),
+                in0=runs(gates[u][:, :, lo:hi]),
+                in1=runs(inputs["att2", u][:, :, lo:hi]),
+                op=ALU.add,
+            )
+
+        def project(u, m, acc, lo=0, hi=W):
+            words, scales = codes["fused", u]
+            nc.tensor.matmul_mx(
+                out=acc,
+                lhsT=wp[:, 2 * P * m : 2 * P * (m + 1)].bitcast(FP4X4),
+                lhsT_scale=scales_raw[:, 2, P * m : P * (m + 1)],
+                rhs=words[:, lo:hi].bitcast(FP8X4),
+                rhs_scale=scales[:, lo:hi],
+                start=True,
+                stop=True,
+            )
+
+        def store(u, m0, m1, lo=0, hi=W):
+            b, h = divmod(u, 2)
+            view = out[b].rearrange("(m p) h w -> p m (h w)", p=P)
+            nc.sync.dma_start(out=view[:, m0:m1, h * W + lo : h * W + hi], in_=ys[u][:, m0:m1, lo:hi])
+
+        def evacuate(u, m, acc, lo=0, hi=W, on_vector=False):
+            if u not in ys:
+                ys[u] = work.tile([P, T, W], F32, name="y")
+            if on_vector:
+                nc.vector.tensor_scalar(out=ys[u][:, m, lo:hi], in0=acc, scalar1=bp_cols[:, m : m + 1], scalar2=None, op0=ALU.add)
+            else:
+                nc.scalar.activation(ys[u][:, m, lo:hi], acc, ACT.Identity, bias=bp_cols[:, m : m + 1])
+
+        last = UNITS - 1
+        for u in range(-2, UNITS):
+            if u == 0:
+                load_batch(2)
+            if u == 2:
+                load_batch(3)
+            for t in range(T):
+                if u + 2 < UNITS:
+                    widen(u + 2, t)
+                if u - 1 >= 0:
+                    y = y_psum.tile([P, W], F32, name="y_acc")
+                    project(u - 1, t, y[:])
+                    evacuate(u - 1, t, y[:])
+                    if t % 2 == 1:
+                        store(u - 1, t - 1, t + 1)
+            if u == -2:
+                wg = keep.tile([P, 2, 2 * C], U8, name="wg", align_bytes=64)
+                for g in (1, 0):
+                    nc.vector.tensor_copy(
+                        out=wg[:, g, :].rearrange("p (t m e) -> p t m e", t=T, e=2),
+                        in_=wg_raw[:, g, :].rearrange("p (m t e) -> p t m e", t=T, e=2),
+                    )
+                interleave_hsi_vector(0)
+            if u >= 0:
+                for t in range(T):
+                    gated(u, t)
+            if u == -1:
+                wg_s = keep.tile([P, 2, C], U8, name="wg_s", align_bytes=64)
+                nc.vector.tensor_copy(
+                    out=wg_s[:].rearrange("p g (t m) -> p g t m", t=T),
+                    in_=scales_raw[:, 0:2, :].rearrange("p g (m t) -> p g t m", t=T),
+                )
+                bg_cols = keep.tile([P, T], F32, name="bg_cols")
+                nc.vector.tensor_copy(out=bg_cols[:], in_=bg_raw[:])
+            if 0 <= u + 1 < UNITS:
+                quantize("hsi", u + 1, inter["hsi", u + 1])
+                for t in range(T):
+                    gate(u + 1, t)
+                for t in range(DIFFS_ON_TENSOR[u + 1]):
+                    diff_tensor(u + 1, t)
+            if u == -1:
+                bp_t = y_psum.tile([P, P], BF16, name="y_acc")
+                nc.tensor.transpose(bp_t[:], bp_rows[:], ident[:])
+            if 0 <= u < last:
+                add_att2(u)
+            if u + 2 < UNITS:
+                interleave("msi", u + 2, nc.vector.tensor_copy, wide[u + 2], 0, W)
+                interleave_hsi_scalar(u + 2)
+            if 0 <= u < last:
+                quantize("fused", u, inter["fused", u])
+            if u + 2 < UNITS:
+                quantize("msi", u + 2, inter["msi", u + 2])
+            if 0 <= u + 1 < UNITS:
+                diff_vector(u + 1)
+            if u >= -1 and u + 2 < UNITS:
+                interleave_hsi_vector(u + 2)
+            if u == -1:
+                bp_cols = keep.tile([P, T], F32, name="bp_cols")
+                nc.vector.tensor_copy(out=bp_cols[:], in_=bp_t[:, 0:T])
+
+        half = W // 2
+        add_att2(last, 0, half)
+        add_att2(last, half, W)
+        quantize("fused", last, inter["fused", last], 0, half)
+        quantize("fused", last, inter["fused", last], half, W)
+        pools = [y_psum, y_psum, gate_psum, gate_psum, gate_psum, diff_psum, diff_psum, diff_psum]
+        names = ["y_acc", "y_acc", "gate_acc", "gate_acc", "gate_acc", "diff_acc", "diff_acc", "diff_acc"]
+        for k in range(2 * T):
+            h, m = divmod(k, T)
+            lo, hi = h * half, (h + 1) * half
+            y = pools[k].tile([P, W], F32, name=names[k])
+            project(last, m, y[:, 0:half], lo, hi)
+            evacuate(last, m, y[:, 0:half], lo, hi, on_vector=(h == 1 and m % 2 == 1))
+            if m % 2 == 1:
+                store(last, m - 1, m + 1, lo, hi)

@@ -22,7 +22,7 @@ T = 4
 W = 512
 UNITS = B * N // W
 RUN = 8
-HSI_ON_SCALAR = 512
+HSI_ON_SCALAR = 352
 DIFFS_ON_TENSOR = [2, 2, 2, 2, 2, 3, 3, 3]
 
 
@@ -216,20 +216,20 @@ def tile_crossattentionfusion_pa_t_w4_kernel(
                 nc.scalar.activation(ys[u][:, m, lo:hi], acc, ACT.Identity, bias=bp_cols[:, m : m + 1])
 
         last = UNITS - 1
-        for u in range(-2, UNITS):
+        for u in range(-3, UNITS):
             if u == 0:
                 load_batch(2)
             if u == 2:
                 load_batch(3)
             for t in range(T):
-                if u + 2 < UNITS:
-                    widen(u + 2, t)
                 if u - 1 >= 0:
                     y = y_psum.tile([P, W], F32, name="y_acc")
                     project(u - 1, t, y[:])
                     evacuate(u - 1, t, y[:])
                     if t % 2 == 1:
                         store(u - 1, t - 1, t + 1)
+            if -2 <= u and u + 2 < UNITS:
+                interleave_hsi_scalar(u + 2)
             if u == -2:
                 wg = keep.tile([P, 2, 2 * C], U8, name="wg", align_bytes=64)
                 for g in (1, 0):
@@ -255,17 +255,19 @@ def tile_crossattentionfusion_pa_t_w4_kernel(
                     gate(u + 1, t)
                 for t in range(DIFFS_ON_TENSOR[u + 1]):
                     diff_tensor(u + 1, t)
+            if u + 3 < UNITS:
+                for t in range(T):
+                    widen(u + 3, t)
             if u == -1:
                 bp_t = y_psum.tile([P, P], BF16, name="y_acc")
                 nc.tensor.transpose(bp_t[:], bp_rows[:], ident[:])
             if 0 <= u < last:
                 add_att2(u)
-            if u + 2 < UNITS:
+            if -2 <= u and u + 2 < UNITS:
                 interleave("msi", u + 2, nc.vector.tensor_copy, wide[u + 2], 0, W)
-                interleave_hsi_scalar(u + 2)
             if 0 <= u < last:
                 quantize("fused", u, inter["fused", u])
-            if u + 2 < UNITS:
+            if -2 <= u and u + 2 < UNITS:
                 quantize("msi", u + 2, inter["msi", u + 2])
             if 0 <= u + 1 < UNITS:
                 diff_vector(u + 1)

@@ -170,11 +170,15 @@ def tile_crossattentionfusion_pa_t_w4_kernel(
             diffs[u, t] = d[:]
 
         def diff_vector(u):
-            n = DIFFS_ON_TENSOR[u]
-            d = work.tile([P, T, W], F32, name="diff_sb")
-            nc.vector.tensor_tensor(out=d[:, n:T, :], in0=inputs["att1", u][:, n:T, :], in1=inputs["att2", u][:, n:T, :], op=ALU.subtract)
-            for t in range(n, T):
-                diffs[u, t] = d[:, t, :]
+            if DIFFS_ON_TENSOR[u] == 2:
+                d = work.tile([P, W], F32, name="diff_v")
+                nc.vector.tensor_tensor(out=d[:], in0=inputs["att1", u][:, 2, :], in1=inputs["att2", u][:, 2, :], op=ALU.subtract)
+                diffs[u, 2] = d[:]
+
+        def diff_gpsimd(u):
+            d = keep.tile([P, W], F32, name="diff_g")
+            nc.gpsimd.tensor_tensor(out=d[:], in0=inputs["att1", u][:, 3, :], in1=inputs["att2", u][:, 3, :], op=ALU.subtract)
+            diffs[u, 3] = d[:]
 
         def gated(u, t):
             g = gates[u][:, t, :]
@@ -239,7 +243,11 @@ def tile_crossattentionfusion_pa_t_w4_kernel(
                     )
                 interleave_hsi_vector(0)
             if u >= 0:
-                for t in range(T):
+                gated(u, 3)
+            if 0 <= u + 1 < UNITS:
+                diff_gpsimd(u + 1)
+            if u >= 0:
+                for t in range(3):
                     gated(u, t)
             if u == -1:
                 wg_s = keep.tile([P, 2, C], U8, name="wg_s", align_bytes=64)

from contextlib import ExitStack

import concourse.mybir as mybir
from concourse.masks import make_identity

BF16 = mybir.dt.bfloat16
F32 = mybir.dt.float32
I32 = mybir.dt.int32
U32 = mybir.dt.uint32
U8 = mybir.dt.uint8
FP8 = mybir.dt.float8_e4m3fn
FP8X4 = mybir.dt.float8_e4m3fn_x4
FP4X4 = mybir.dt.float4_e2m1fn_x4
ACT = mybir.ActivationFunctionType
ALU = mybir.AluOpType

B, C, N = 4, 512, 1024
FLOPS = 2 * B * N * (2 * C * C + C * C)

P = 128
T = 4
W = 512
UNITS = B * N // W
RUN = 8
HSI_ON_SCALAR = 352
DIFFS_ON_TENSOR = [2, 2, 2, 2, 2, 3, 3, 3]


def tile_crossattentionfusion_pa_t_w4_kernel(
    tc, hsi, msi_bytes, msi_scale, att1, att2, wg_words, wg_scales, bg, wp_words, wp_scales, bp, out
):
    nc = tc.nc

    def channels_first(x, b):
        return x[b].rearrange("(p t) h w -> p t (h w)", t=T)

    with ExitStack() as ctx:
        keep = ctx.enter_context(tc.tile_pool(name="keep", bufs=1))
        work = ctx.enter_context(tc.tile_pool(name="work", bufs=2))
        gate_psum = ctx.enter_context(tc.psum_pool(name="gate_psum", bufs=3))
        diff_psum = ctx.enter_context(tc.psum_pool(name="diff_psum", bufs=3))
        y_psum = ctx.enter_context(tc.psum_pool(name="y_psum", bufs=2))
        ctx.enter_context(tc.manual_schedule())

        warm = keep.tile([P, 1], F32, name="warm")
        nc.vector.memset(warm[:], 0.0)
        nc.scalar.activation(warm[:], warm[:], ACT.Sigmoid)
        scales_raw = keep.tile([P, 3, C], U8, name="scales_raw", align_bytes=64)
        nc.vector.memset(scales_raw[:].rearrange("p g n -> p (g n)").bitcast(I32), 0)
        bp_rows = keep.tile([P, P], BF16, name="bp_rows")
        nc.gpsimd.memset(bp_rows[:], 0.0)
        ident = keep.tile([P, P], BF16, name="ident")
        make_identity(nc, ident[:])
        neg_ident = keep.tile([P, P], BF16, name="neg_ident")
        nc.vector.tensor_scalar(out=neg_ident[:], in0=ident[:], scalar1=-1.0, scalar2=None, op0=ALU.mult)

        inputs = {}

        def load(name, src, b, halves, dtype):
            view = channels_first(src, b)
            if halves is None:
                whole = keep.tile([P, T, N], dtype, name=f"{name}_{b}")
                nc.sync.dma_start(out=whole[:], in_=view)
                for h in range(2):
                    inputs[name, 2 * b + h] = whole[:, :, h * W : (h + 1) * W]
            else:
                for h in halves:
                    half = keep.tile([P, T, W], dtype, name=f"{name}_{b}_{h}")
                    nc.sync.dma_start(out=half[:], in_=view[:, :, h * W : (h + 1) * W])
                    inputs[name, 2 * b + h] = half[:]

        def load_batch(b):
            load("msi", msi_bytes, b, None, U8)
            load("hsi", hsi, b, None, BF16)
            load("att1", att1, b, None, BF16)
            load("att2", att2, b, None, BF16)

        m_scale = keep.tile([P, T], F32, name="m_scale")
        nc.sync.dma_start(out=m_scale[:], in_=msi_scale.rearrange("a (p t) b c -> p (a t b c)", t=T))
        load("msi", msi_bytes, 0, (0,), U8)
        wg_raw = keep.tile([P, 2, 2 * C], U8, name="wg_raw", align_bytes=64)
        nc.sync.dma_start(out=wg_raw[:], in_=wg_words.rearrange("g p n -> p g n"))
        load("hsi", hsi, 0, (0,), BF16)
        for q in range(4):
            nc.sync.dma_start(
                out=scales_raw[32 * q : 32 * q + 4, 0:2, :].bitcast(I32),
                in_=wg_scales[:, 4 * q : 4 * q + 4, :].rearrange("g q n -> q g n").bitcast(I32),
            )
        bg_raw = keep.tile([P, T], BF16, name="bg_raw")
        nc.sync.dma_start(out=bg_raw[:], in_=bg.rearrange("(p t) -> p t", t=T))
        load("msi", msi_bytes, 0, (1,), U8)
        load("hsi", hsi, 0, (1,), BF16)
        load("att1", att1, 0, (0,), BF16)
        load("att2", att2, 0, (0,), BF16)
        nc.sync.dma_start(out=bp_rows[0:4, :], in_=bp.rearrange("(m p) -> m p", p=P))
        wp = keep.tile([P, 2 * C], U8, name="wp", align_bytes=64)
        nc.sync.dma_start(out=wp[:], in_=wp_words[0])
        for q in range(4):
            nc.sync.dma_start(
                out=scales_raw[32 * q : 32 * q + 4, 2, :].bitcast(I32),
                in_=wp_scales[0, 4 * q : 4 * q + 4, :].bitcast(I32),
            )
        load("att1", att1, 0, (1,), BF16)
        load("att2", att2, 0, (1,), BF16)
        load_batch(1)

        wide, inter, codes, gates, diffs, ys = {}, {}, {}, {}, {}, {}

        def widen(u, t):
            if t == 0:
                wide[u] = work.tile([P, T, W], BF16, name="wide")
            src = inputs["msi", u][:, t, :].bitcast(FP8)
            if u == 0 and t >= 2:
                nc.vector.tensor_scalar(out=wide[u][:, t, :], in0=src, scalar1=m_scale[:, t : t + 1], scalar2=None, op0=ALU.mult)
            else:
                nc.scalar.activation(wide[u][:, t, :], src, ACT.Copy, scale=m_scale[:, t : t + 1])

        def by_runs(grouped, px):
            return grouped.rearrange("p (c i t) -> p c t i", i=RUN, t=T)

        def runs(planar):
            return planar.rearrange("p t (c i) -> p c t i", i=RUN)

        def interleave(name, u, copy, planar, lo, hi):
            if (name, u) not in inter:
                inter[name, u] = work.tile([P, T * W], BF16, name=f"inter_{name}", align_bytes=64)
            copy(
                out=by_runs(inter[name, u][:, T * lo : T * hi], hi - lo),
                in_=runs(planar[:, :, lo:hi]),
            )

        def interleave_hsi_scalar(u):
            if u > 0:
                interleave("hsi", u, nc.scalar.copy, inputs["hsi", u], 0, HSI_ON_SCALAR)

        def interleave_hsi_vector(u):
            lo = HSI_ON_SCALAR if u > 0 else 0
            if lo < W:
                interleave("hsi", u, nc.vector.tensor_copy, inputs["hsi", u], lo, W)

        def quantize(name, u, src, lo=0, hi=W):
            if (name, u) not in codes:
                words = work.tile([P, W], U32, name=f"codes_{name}", align_bytes=64)
                scales = work.tile([P, W], U8, name=f"scales_{name}", align_bytes=64)
                codes[name, u] = (words, scales)
            words, scales = codes[name, u]
            nc.vector.quantize_mx(out=words[:, lo:hi].bitcast(FP8X4), scales=scales[:, lo:hi], in_=src[:, T * lo : T * hi])

        def gate(u, t):
            acc = gate_psum.tile([P, W], F32, name="gate_acc")
            for g, name in ((1, "msi"), (0, "hsi")):
                words, scales = codes[name, u]
                nc.tensor.matmul_mx(
                    out=acc[:],
                    lhsT=wg[:, g, 2 * P * t : 2 * P * (t + 1)].bitcast(FP4X4),
                    lhsT_scale=wg_s[:, g, P * t : P * (t + 1)],
                    rhs=words[:].bitcast(FP8X4),
                    rhs_scale=scales[:],
                    start=(g == 1),
                    stop=(g == 0),
                )
            if t == 0:
                gates[u] = work.tile([P, T, W], F32, name="gates")
            nc.scalar.activation(gates[u][:, t, :], acc[:], ACT.Sigmoid, bias=bg_cols[:, t : t + 1])

        def diff_tensor(u, t):
            d = diff_psum.tile([P, W], F32, name="diff_acc")
            nc.tensor.matmul(d[:], ident[:], inputs["att1", u][:, t, :], start=True, stop=False)
            nc.tensor.matmul(d[:], neg_ident[:], inputs["att2", u][:, t, :], start=False, stop=True)
            diffs[u, t] = d[:]

        def diff_vector(u):
            if DIFFS_ON_TENSOR[u] == 2:
                d = work.tile([P, W], F32, name="diff_v")
                nc.vector.tensor_tensor(out=d[:], in0=inputs["att1", u][:, 2, :], in1=inputs["att2", u][:, 2, :], op=ALU.subtract)
                diffs[u, 2] = d[:]

        def diff_gpsimd(u):
            d = keep.tile([P, W], F32, name="diff_g")
            nc.gpsimd.tensor_tensor(out=d[:], in0=inputs["att1", u][:, 3, :], in1=inputs["att2", u][:, 3, :], op=ALU.subtract)
            diffs[u, 3] = d[:]

        def gated(u, t):
            g = gates[u][:, t, :]
            nc.vector.tensor_tensor(out=g, in0=diffs[u, t], in1=g, op=ALU.mult)

        def add_att2(u, lo=0, hi=W):
            if ("fused", u) not in inter:
                inter["fused", u] = work.tile([P, T * W], BF16, name="fused", align_bytes=64)
            nc.vector.tensor_tensor(
                out=by_runs(inter["fused", u][:, T * lo : T * hi], hi - lo),
                in0=runs(gates[u][:, :, lo:hi]),
                in1=runs(inputs["att2", u][:, :, lo:hi]),
                op=ALU.add,
            )

        def project(u, m, acc, lo=0, hi=W):
            words, scales = codes["fused", u]
            nc.tensor.matmul_mx(
                out=acc,
                lhsT=wp[:, 2 * P * m : 2 * P * (m + 1)].bitcast(FP4X4),
                lhsT_scale=scales_raw[:, 2, P * m : P * (m + 1)],
                rhs=words[:, lo:hi].bitcast(FP8X4),
                rhs_scale=scales[:, lo:hi],
                start=True,
                stop=True,
            )

        def store(u, m0, m1, lo=0, hi=W):
            b, h = divmod(u, 2)
            view = out[b].rearrange("(m p) h w -> p m (h w)", p=P)
            nc.sync.dma_start(out=view[:, m0:m1, h * W + lo : h * W + hi], in_=ys[u][:, m0:m1, lo:hi])

        def evacuate(u, m, acc, lo=0, hi=W, on_vector=False):
            if u not in ys:
                ys[u] = work.tile([P, T, W], F32, name="y")
            if on_vector:
                nc.vector.tensor_scalar(out=ys[u][:, m, lo:hi], in0=acc, scalar1=bp_cols[:, m : m + 1], scalar2=None, op0=ALU.add)
            else:
                nc.scalar.activation(ys[u][:, m, lo:hi], acc, ACT.Identity, bias=bp_cols[:, m : m + 1])

        last = UNITS - 1
        for u in range(-3, UNITS):
            if u == 0:
                load_batch(2)
            if u == 2:
                load_batch(3)
            for t in range(T):
                if u - 1 >= 0:
                    y = y_psum.tile([P, W], F32, name="y_acc")
                    project(u - 1, t, y[:])
                    evacuate(u - 1, t, y[:])
                    if t % 2 == 1:
                        store(u - 1, t - 1, t + 1)
            if -2 <= u and u + 2 < UNITS:
                interleave_hsi_scalar(u + 2)
            if u == -2:
                wg = keep.tile([P, 2, 2 * C], U8, name="wg", align_bytes=64)
                for g in (1, 0):
                    nc.vector.tensor_copy(
                        out=wg[:, g, :].rearrange("p (t m e) -> p t m e", t=T, e=2),
                        in_=wg_raw[:, g, :].rearrange("p (m t e) -> p t m e", t=T, e=2),
                    )
                interleave_hsi_vector(0)
            if u >= 0:
                gated(u, 3)
            if 0 <= u + 1 < UNITS:
                diff_gpsimd(u + 1)
            if u >= 0:
                for t in range(3):
                    gated(u, t)
            if u == -1:
                wg_s = keep.tile([P, 2, C], U8, name="wg_s", align_bytes=64)
                nc.vector.tensor_copy(
                    out=wg_s[:].rearrange("p g (t m) -> p g t m", t=T),
                    in_=scales_raw[:, 0:2, :].rearrange("p g (m t) -> p g t m", t=T),
                )
                bg_cols = keep.tile([P, T], F32, name="bg_cols")
                nc.vector.tensor_copy(out=bg_cols[:], in_=bg_raw[:])
            if 0 <= u + 1 < UNITS:
                quantize("hsi", u + 1, inter["hsi", u + 1])
                for t in range(T):
                    gate(u + 1, t)
                for t in range(DIFFS_ON_TENSOR[u + 1]):
                    diff_tensor(u + 1, t)
            if u + 3 < UNITS:
                for t in range(T):
                    widen(u + 3, t)
            if u == -1:
                bp_t = y_psum.tile([P, P], BF16, name="y_acc")
                nc.tensor.transpose(bp_t[:], bp_rows[:], ident[:])
            if 0 <= u < last:
                add_att2(u)
            if -2 <= u and u + 2 < UNITS:
                interleave("msi", u + 2, nc.vector.tensor_copy, wide[u + 2], 0, W)
            if 0 <= u < last:
                quantize("fused", u, inter["fused", u])
            if -2 <= u and u + 2 < UNITS:
                quantize("msi", u + 2, inter["msi", u + 2])
            if 0 <= u + 1 < UNITS:
                diff_vector(u + 1)
            if u >= -1 and u + 2 < UNITS:
                interleave_hsi_vector(u + 2)
            if u == -1:
                bp_cols = keep.tile([P, T], F32, name="bp_cols")
                nc.vector.tensor_copy(out=bp_cols[:], in_=bp_t[:, 0:T])

        half = W // 2
        add_att2(last, 0, half)
        add_att2(last, half, W)
        quantize("fused", last, inter["fused", last], 0, half)
        quantize("fused", last, inter["fused", last], half, W)
        pools = [y_psum, y_psum, gate_psum, gate_psum, gate_psum, diff_psum, diff_psum, diff_psum]
        names = ["y_acc", "y_acc", "gate_acc", "gate_acc", "gate_acc", "diff_acc", "diff_acc", "diff_acc"]
        for k in range(2 * T):
            h, m = divmod(k, T)
            lo, hi = h * half, (h + 1) * half
            y = pools[k].tile([P, W], F32, name=names[k])
            project(last, m, y[:, 0:half], lo, hi)
            evacuate(last, m, y[:, 0:half], lo, hi, on_vector=(h == 1 and m % 2 == 1))
            if m % 2 == 1:
                store(last, m - 1, m + 1, lo, hi)
